import numpy as np
import ml_dtypes


def mxq(x, axis, fmt="e4m3"):
    dtype, down = {"e4m3": (ml_dtypes.float8_e4m3fn, 7), "e5m2": (ml_dtypes.float8_e5m2, 14)}[fmt]
    v = np.moveaxis(np.asarray(x, np.float32).astype(ml_dtypes.bfloat16).astype(np.float64), axis, -1)
    blocks = v.reshape(v.shape[:-1] + (-1, 32))
    amax = np.abs(blocks).max(-1, keepdims=True)
    byte = np.maximum(np.where(amax > 0, np.frexp(amax)[1] - 1 + 127, 0) - down, 1)
    scale = np.exp2(byte - 127.0)
    codes = (blocks / scale).astype(np.float32).astype(dtype).astype(np.float64)
    return np.moveaxis((codes * scale).reshape(v.shape), -1, axis)


WIDE = False


def mx_kscale(k):
    if not WIDE:
        return np.ones(k)
    levels = np.array([10, -10, 5, -5, 0])
    a = np.random.permutation(np.resize(levels, k // 512 * 4)).reshape(k // 512, 4)
    idx = np.arange(k)
    return np.exp2(a[idx // 512, idx % 128 // 32])


BF16 = ml_dtypes.bfloat16


def bf(x):
    return np.asarray(x, np.float32).astype(BF16)


def f64(x):
    return np.asarray(x).astype(np.float64)


BATCH, IN_FEATURES, OUT_BY_WIN, WIN_SIZE, STRIDE = 1024, 2048, 16, 64, 16
N_WIN = -(-IN_FEATURES // STRIDE)
OUT_FEATURES = N_WIN * OUT_BY_WIN


def build_mask():
    offset = WIN_SIZE // 2
    k = np.arange(N_WIN)
    lo = np.maximum(k * STRIDE - offset, 0)
    hi = k * STRIDE + WIN_SIZE - offset
    j = np.arange(IN_FEATURES)
    win_mask = (j[None, :] >= lo[:, None]) & (j[None, :] < hi[:, None])
    return np.repeat(win_mask, OUT_BY_WIN, axis=0).astype(np.float64)


def setup_inputs():
    s = mx_kscale(IN_FEATURES)
    mask = build_mask()
    bound = np.sqrt(3.0 / WIN_SIZE)
    W = np.random.uniform(-bound, bound, (OUT_FEATURES, IN_FEATURES)) * mask
    return {"x": bf(np.random.standard_normal((BATCH, IN_FEATURES)) * s), "W": bf(W / s[None, :]),
            "b": bf(np.random.uniform(-0.5, 0.5, OUT_FEATURES)), "mask": bf(mask)}


def reference(x, W, b, mask):
    return (mxq(f64(x), 1, "e4m3") @ mxq(f64(W), 1, "e4m3").T) + f64(b)

@@ -1,0 +1,160 @@
+import concourse.mybir as mybir
+from concourse.masks import make_identity
+
+F32 = mybir.dt.float32
+BF16 = mybir.dt.bfloat16
+U32 = mybir.dt.uint32
+U8 = mybir.dt.uint8
+FP8X4 = mybir.dt.float8_e4m3fn_x4
+ADD = mybir.AluOpType.add
+
+P = 128
+BATCH = 1024
+IN_F = 2048
+OUT_F = 2048
+WIN = 64
+N_M = BATCH // P
+N_G = IN_F // 512
+N_OB = OUT_F // P
+
+FLOPS = 2 * BATCH * OUT_F * WIN
+BYTES = BATCH * IN_F * 2 + OUT_F * WIN * 2 + OUT_F * 2 + BATCH * OUT_F * 4
+
+
+def first_chunk(ob):
+    return (ob - 1) // 2
+
+
+def tile_locallayer_kernel(tc, x, W, b, mask, out):
+    nc = tc.nc
+    with tc.tile_pool(name="const", bufs=1) as const, \
+         tc.tile_pool(name="xin", bufs=N_M) as xin, \
+         tc.tile_pool(name="xgp", bufs=3) as xgp, \
+         tc.tile_pool(name="xqp", bufs=N_M) as xqp, \
+         tc.tile_pool(name="wp", bufs=1) as wp, \
+         tc.tile_pool(name="op", bufs=3) as op, \
+         tc.psum_pool(name="pt", bufs=4) as pt, \
+         tc.psum_pool(name="po", bufs=4) as po:
+
+        w_sb = wp.tile([P, N_OB * 512], BF16)
+        w_f = w_sb[:].bitcast(F32)
+        w_pairs = w_f.rearrange("p (i w) -> p i w", w=512)
+        nc.vector.memset(w_pairs[:, :, 0:112], 0.0)
+        nc.vector.memset(w_pairs[:, :, 200:304], 0.0)
+        nc.vector.memset(w_pairs[:, :, 392:512], 0.0)
+        zero = const.tile([P, P], F32)
+        nc.vector.memset(zero[:], 0.0)
+        ones = const.tile([P, P], BF16)
+        nc.vector.memset(ones[:], 1.0)
+        brow = const.tile([P, OUT_F], BF16)
+        nc.vector.memset(brow[:].bitcast(F32), 0.0)
+        ident = const.tile([P, P], F32)
+        make_identity(nc, ident[:])
+
+        def load_w(ob):
+            lo = max(P * ob - 32, 0)
+            hi = min(P * ob + 144, IN_F)
+            k0 = 256 * first_chunk(ob)
+            nc.sync.dma_start(
+                out=w_sb[:, 512 * ob + lo - k0: 512 * ob + hi - k0],
+                in_=W[P * ob: P * ob + P, lo:hi],
+            )
+
+        x_sb = []
+
+        def load_x(m):
+            t = xin.tile([P, IN_F], BF16, name="x_sb")
+            nc.sync.dma_start(out=t[:], in_=x[P * m: P * m + P, :])
+            x_sb.append(t)
+
+        for ob in range(0, 6):
+            load_w(ob)
+        load_x(0)
+        for ob in range(6, N_OB):
+            load_w(ob)
+        load_x(1)
+        nc.sync.dma_start(out=brow[0:1, :], in_=b.unsqueeze(0))
+        for m in range(2, N_M):
+            load_x(m)
+
+        wq = []
+        ws = []
+        n_copy = 0
+        for g in range(N_G):
+            wg = wp.tile([P, 3072], BF16, name="wg%d" % g, align_bytes=64)
+            wg_f = wg[:].bitcast(F32).rearrange("p (o u) -> p o u", u=2)
+            q = wp.tile([P, 768], U32, name="wq%d" % g, align_bytes=64)
+            s = wp.tile([P, 768], U8, name="ws%d" % g, align_bytes=64)
+            wq.append(q)
+            ws.append(s)
+            for pr in range(3):
+                obs = [4 * g - 1 + 2 * pr, 4 * g + 2 * pr]
+                valid = [i for i in range(2) if 0 <= obs[i] < N_OB]
+                c_lo = P * valid[0]
+                c_hi = P * (valid[-1] + 1)
+                bank = pt.tile([P, 512], F32, name="tp")
+                for u in range(2):
+                    for i in valid:
+                        j = 2 * g + u - first_chunk(obs[i])
+                        src = w_f[:, 256 * obs[i] + P * j: 256 * obs[i] + P * j + P] if j in (0, 1) else zero[:]
+                        nc.tensor.transpose(bank[:, 256 * u + P * i: 256 * u + P * i + P], src, ident[:])
+                dst = wg_f[:, 256 * pr + c_lo: 256 * pr + c_hi, :]
+                srcv = bank[:].rearrange("p (u o) -> p o u", u=2)[:, c_lo:c_hi, :]
+                if n_copy % 2 == 0:
+                    nc.scalar.copy(out=dst, in_=srcv)
+                else:
+                    nc.vector.tensor_copy(out=dst, in_=srcv)
+                n_copy += 1
+                nc.vector.quantize_mx(
+                    out=q[:, 256 * pr + c_lo: 256 * pr + c_hi].bitcast(FP8X4),
+                    scales=s[:, 256 * pr + c_lo: 256 * pr + c_hi],
+                    in_=wg[:, 4 * (256 * pr + c_lo): 4 * (256 * pr + c_hi)],
+                )
+
+        bias = const.tile([P, OUT_F], F32)
+        for g in range(N_G):
+            acc = po.tile([P, 512], F32, name="acc")
+            nc.tensor.matmul(out=acc[:], lhsT=ones[:], rhs=brow[:, 512 * g: 512 * g + 512], start=True, stop=True)
+            nc.scalar.copy(out=bias[:, 512 * g: 512 * g + 512], in_=acc[:])
+
+        for m in range(N_M):
+            x_f = x_sb[m][:].bitcast(F32)
+            xg = xgp.tile([P, IN_F], BF16, name="xg", align_bytes=64)
+            xg_f = xg[:].bitcast(F32).rearrange("p (g r u) -> p g r u", g=N_G, u=2)
+            for h in range(2):
+                bank = pt.tile([P, 512], F32, name="tp")
+                for c in range(4):
+                    nc.tensor.transpose(bank[:, P * c: P * c + P], x_f[:, 512 * h + P * c: 512 * h + P * c + P], ident[:])
+                nc.scalar.copy(
+                    out=xg_f[:, 2 * h: 2 * h + 2, :, :],
+                    in_=bank[:].rearrange("p (g u r) -> p g r u", g=2, u=2),
+                )
+            xq = xqp.tile([P, 512], U32, name="xq", align_bytes=64)
+            xs = xqp.tile([P, 512], U8, name="xs", align_bytes=64)
+            nc.vector.quantize_mx(out=xq[:].bitcast(FP8X4), scales=xs[:], in_=xg[:])
+
+            def mx(dst, gx, gw, c0, n, start, stop):
+                nc.tensor.matmul_mx(
+                    out=dst,
+                    lhsT=xq[:, P * gx: P * gx + P].bitcast(FP8X4),
+                    lhsT_scale=xs[:, P * gx: P * gx + P],
+                    rhs=wq[gw][:, c0: c0 + n].bitcast(FP8X4),
+                    rhs_scale=ws[gw][:, c0: c0 + n],
+                    start=start,
+                    stop=stop,
+                )
+
+            ot = op.tile([P, OUT_F], F32, name="ot")
+            for g in range(N_G):
+                acc = po.tile([P, 512], F32, name="acc")
+                mx(acc[:, 0:128], g, g, 128, 128, True, g == 0)
+                if g > 0:
+                    mx(acc[:, 0:128], g - 1, g - 1, 640, 128, False, True)
+                mx(acc[:, 128:384], g, g, 256, 256, True, True)
+                mx(acc[:, 384:512], g, g, 512, 128, True, g == N_G - 1)
+                if g < N_G - 1:
+                    mx(acc[:, 384:512], g + 1, g + 1, 0, 128, False, True)
+                nc.vector.tensor_tensor(
+                    out=ot[:, 512 * g: 512 * g + 512], in0=acc[:], in1=bias[:, 512 * g: 512 * g + 512], op=ADD
+                )
+            nc.sync.dma_start(out=out[P * m: P * m + P, :], in_=ot[:])

@@ -2,6 +2,7 @@ import concourse.mybir as mybir
 from concourse.masks import make_identity
 
 F32 = mybir.dt.float32
+I32 = mybir.dt.int32
 BF16 = mybir.dt.bfloat16
 U32 = mybir.dt.uint32
 U8 = mybir.dt.uint8
@@ -16,13 +17,14 @@ WIN = 64
 N_M = BATCH // P
 N_G = IN_F // 512
 N_OB = OUT_F // P
+WCOL = 768
 
 FLOPS = 2 * BATCH * OUT_F * WIN
 BYTES = BATCH * IN_F * 2 + OUT_F * WIN * 2 + OUT_F * 2 + BATCH * OUT_F * 4
 
-
-def first_chunk(ob):
-    return (ob - 1) // 2
+VIA_SCALAR = [(m, 0) for m in range(1, N_M)]
+M_RING = ["k3", "k4", "k7", "k0"]
+X_RING = ["k5", "k6", "k1", "k2"]
 
 
 def tile_locallayer_kernel(tc, x, W, b, mask, out):
@@ -30,35 +32,35 @@ def tile_locallayer_kernel(tc, x, W, b, mask, out):
     with tc.tile_pool(name="const", bufs=1) as const, \
          tc.tile_pool(name="xin", bufs=N_M) as xin, \
          tc.tile_pool(name="xgp", bufs=3) as xgp, \
-         tc.tile_pool(name="xqp", bufs=N_M) as xqp, \
-         tc.tile_pool(name="wp", bufs=1) as wp, \
-         tc.tile_pool(name="op", bufs=3) as op, \
-         tc.psum_pool(name="pt", bufs=4) as pt, \
-         tc.psum_pool(name="po", bufs=4) as po:
+         tc.tile_pool(name="xqp", bufs=4) as xqp, \
+         tc.tile_pool(name="op", bufs=4) as op, \
+         tc.psum_pool(name="ps", bufs=1) as ps, \
+         tc.manual_schedule():
 
-        w_sb = wp.tile([P, N_OB * 512], BF16)
+        w_sb = const.tile([P, 17 * 512], BF16)
         w_f = w_sb[:].bitcast(F32)
-        w_pairs = w_f.rearrange("p (i w) -> p i w", w=512)
-        nc.vector.memset(w_pairs[:, :, 0:112], 0.0)
-        nc.vector.memset(w_pairs[:, :, 200:304], 0.0)
-        nc.vector.memset(w_pairs[:, :, 392:512], 0.0)
+        wg = const.tile([P, N_G * WCOL * 4], BF16, align_bytes=64)
+        wg_f = wg[:].bitcast(F32).rearrange("p (o u) -> p o u", u=2)
+        wq = const.tile([P, N_G * WCOL], U32, align_bytes=64)
+        ws = const.tile([P, N_G * WCOL], U8, align_bytes=64)
         zero = const.tile([P, P], F32)
-        nc.vector.memset(zero[:], 0.0)
         ones = const.tile([P, P], BF16)
-        nc.vector.memset(ones[:], 1.0)
         brow = const.tile([P, OUT_F], BF16)
-        nc.vector.memset(brow[:].bitcast(F32), 0.0)
+        bias = const.tile([P, OUT_F], BF16)
         ident = const.tile([P, P], F32)
-        make_identity(nc, ident[:])
 
-        def load_w(ob):
-            lo = max(P * ob - 32, 0)
-            hi = min(P * ob + 144, IN_F)
-            k0 = 256 * first_chunk(ob)
-            nc.sync.dma_start(
-                out=w_sb[:, 512 * ob + lo - k0: 512 * ob + hi - k0],
-                in_=W[P * ob: P * ob + P, lo:hi],
-            )
+        nc.vector.memset(brow[:].bitcast(F32), 0.0)
+        nc.sync.dma_start(out=brow[0:1, :], in_=b.unsqueeze(0))
+        w_flat = W.rearrange("a b -> (a b)")
+        pitch = P * IN_F + P
+
+        def load_w(first, n):
+            src = w_flat[first * pitch - 32: first * pitch - 32 + n * pitch]
+            src = src.rearrange("(i l) -> i l", l=pitch)[:, 0: P * IN_F]
+            src = src.rearrange("i (p q) -> p i q", q=IN_F)[:, :, 0:176]
+            dst = w_sb[:, 512 * first + 224: 512 * first + 224 + 512 * n]
+            dst = dst.rearrange("p (i c) -> p i c", c=512)[:, :, 0:176]
+            nc.sync.dma_start(out=dst, in_=src)
 
         x_sb = []
 
@@ -67,94 +69,189 @@ def tile_locallayer_kernel(tc, x, W, b, mask, out):
             nc.sync.dma_start(out=t[:], in_=x[P * m: P * m + P, :])
             x_sb.append(t)
 
-        for ob in range(0, 6):
-            load_w(ob)
+        nc.sync.dma_start(out=w_sb[:, 256:400], in_=W[0:P, 0:144])
+        load_w(1, 6)
         load_x(0)
-        for ob in range(6, N_OB):
-            load_w(ob)
-        load_x(1)
-        nc.sync.dma_start(out=brow[0:1, :], in_=b.unsqueeze(0))
-        for m in range(2, N_M):
+        load_w(7, 8)
+        nc.sync.dma_start(out=w_sb[:, 512 * 15 + 224: 512 * 15 + 384], in_=W[15 * P: 16 * P, IN_F - 160: IN_F])
+        for m in range(1, N_M):
             load_x(m)
 
-        wq = []
-        ws = []
-        n_copy = 0
-        for g in range(N_G):
-            wg = wp.tile([P, 3072], BF16, name="wg%d" % g, align_bytes=64)
-            wg_f = wg[:].bitcast(F32).rearrange("p (o u) -> p o u", u=2)
-            q = wp.tile([P, 768], U32, name="wq%d" % g, align_bytes=64)
-            s = wp.tile([P, 768], U8, name="ws%d" % g, align_bytes=64)
-            wq.append(q)
-            ws.append(s)
-            for pr in range(3):
-                obs = [4 * g - 1 + 2 * pr, 4 * g + 2 * pr]
-                valid = [i for i in range(2) if 0 <= obs[i] < N_OB]
-                c_lo = P * valid[0]
-                c_hi = P * (valid[-1] + 1)
-                bank = pt.tile([P, 512], F32, name="tp")
-                for u in range(2):
-                    for i in valid:
-                        j = 2 * g + u - first_chunk(obs[i])
-                        src = w_f[:, 256 * obs[i] + P * j: 256 * obs[i] + P * j + P] if j in (0, 1) else zero[:]
-                        nc.tensor.transpose(bank[:, 256 * u + P * i: 256 * u + P * i + P], src, ident[:])
-                dst = wg_f[:, 256 * pr + c_lo: 256 * pr + c_hi, :]
-                srcv = bank[:].rearrange("p (u o) -> p o u", u=2)[:, c_lo:c_hi, :]
-                if n_copy % 2 == 0:
-                    nc.scalar.copy(out=dst, in_=srcv)
-                else:
-                    nc.vector.tensor_copy(out=dst, in_=srcv)
-                n_copy += 1
-                nc.vector.quantize_mx(
-                    out=q[:, 256 * pr + c_lo: 256 * pr + c_hi].bitcast(FP8X4),
-                    scales=s[:, 256 * pr + c_lo: 256 * pr + c_hi],
-                    in_=wg[:, 4 * (256 * pr + c_lo): 4 * (256 * pr + c_hi)],
-                )
+        make_identity(nc, ident[:])
+        nc.vector.memset(ones[:], 1.0)
+        nc.vector.memset(zero[:], 0.0)
+        nc.vector.memset(w_f[:, 200: 200 + 16 * 256].rearrange("p (i w) -> p i w", w=256)[:, :, 0:168], 0.0)
+        nc.vector.memset(
+            wq[:].bitcast(I32)[:, 704: 704 + 3 * WCOL].rearrange("p (g c) -> p g c", c=WCOL)[:, :, 0:128], 0)
+        nc.vector.memset(
+            ws[:].bitcast(I32)[:, 176: 176 + 3 * 192].rearrange("p (g c) -> p g c", c=192)[:, :, 0:32], 0)
 
-        bias = const.tile([P, OUT_F], F32)
-        for g in range(N_G):
-            acc = po.tile([P, 512], F32, name="acc")
-            nc.tensor.matmul(out=acc[:], lhsT=ones[:], rhs=brow[:, 512 * g: 512 * g + 512], start=True, stop=True)
-            nc.scalar.copy(out=bias[:, 512 * g: 512 * g + 512], in_=acc[:])
+        for h in range(2):
+            bb = ps.tile([P, 1024], BF16, name=M_RING[h])
+            for i in range(2):
+                nc.tensor.matmul(out=bb[:, 512 * i: 512 * i + 512], lhsT=ones[:],
+                                 rhs=brow[:, 1024 * h + 512 * i: 1024 * h + 512 * i + 512], start=True, stop=True)
+            nc.scalar.copy(out=bias[:, 1024 * h: 1024 * h + 1024], in_=bb[:])
 
-        for m in range(N_M):
+        def window(ob, chunk):
+            j = chunk - (ob - 1) // 2
+            base = 256 * ob + 64 * (ob % 2) + P * j
+            return w_f[:, base: base + P]
+
+        bank_a = ps.tile([P, 512], F32, name="k0")
+        bank_b = ps.tile([P, 512], F32, name="k1")
+        bank_c = ps.tile([P, 512], F32, name="k2")
+        for i in range(2):
+            nc.tensor.transpose(bank_a[:, 256 + P * i: 256 + P * i + P], zero[:], ident[:])
+            nc.tensor.transpose(bank_c[:, P * i: P * i + P], zero[:], ident[:])
+
+        def quant_w(g, c0, c1):
+            lo = WCOL * g + c0
+            hi = WCOL * g + c1
+            nc.vector.quantize_mx(out=wq[:, lo:hi].bitcast(FP8X4), scales=ws[:, lo:hi], in_=wg[:, 4 * lo: 4 * hi])
+
+        def w_copy(eng_copy, g, bank, col0, lo, hi):
+            eng_copy(out=wg_f[:, WCOL * g + col0 + lo: WCOL * g + col0 + hi, :],
+                     in_=bank[:].rearrange("p (u o) -> p o u", u=2)[:, lo:hi, :])
+
+        def w_t(g):
+            if g > 0:
+                nc.tensor.transpose(bank_a[:, 0:P], window(4 * g - 1, 2 * g), ident[:])
+            nc.tensor.transpose(bank_a[:, P:256], window(4 * g, 2 * g), ident[:])
+            for u in range(2):
+                for i in range(2):
+                    nc.tensor.transpose(bank_b[:, 256 * u + P * i: 256 * u + P * i + P],
+                                        window(4 * g + 1 + i, 2 * g + u), ident[:])
+            nc.tensor.transpose(bank_c[:, 256:384], window(4 * g + 3, 2 * g + 1), ident[:])
+            if g < N_G - 1:
+                nc.tensor.transpose(bank_c[:, 384:512], window(4 * g + 4, 2 * g + 1), ident[:])
+
+        def w_c(g):
+            w_copy(nc.scalar.copy, g, bank_a, 0, 64 if g > 0 else 128, 256)
+            w_copy(nc.vector.tensor_copy, g, bank_c, 512, 0, 192 if g < N_G - 1 else 128)
+            w_copy(nc.scalar.copy, g, bank_b, 256, 0, 256)
+
+        def w_q(g):
+            if g > 0:
+                quant_w(g, 64, 128)
+            quant_w(g, 128, 256)
+            quant_w(g, 512, 640)
+            if g < N_G - 1:
+                quant_w(g, 640, 704)
+            quant_w(g, 256, 512)
+
+        x_banks = {}
+        x_q = {}
+        x_g = {}
+
+        def xt(m):
             x_f = x_sb[m][:].bitcast(F32)
+            x_banks[m] = []
+            for h in range(2):
+                bank = ps.tile([P, 512], F32, name=X_RING[h + (2 if (m % 2 == 0 and m >= 2) else 0)])
+                for c in range(4):
+                    nc.tensor.transpose(bank[:, P * c: P * c + P], x_f[:, 512 * h + P * c: 512 * h + P * c + P], ident[:])
+                x_banks[m].append(bank)
+
+        def xc(m):
             xg = xgp.tile([P, IN_F], BF16, name="xg", align_bytes=64)
             xg_f = xg[:].bitcast(F32).rearrange("p (g r u) -> p g r u", g=N_G, u=2)
             for h in range(2):
-                bank = pt.tile([P, 512], F32, name="tp")
-                for c in range(4):
-                    nc.tensor.transpose(bank[:, P * c: P * c + P], x_f[:, 512 * h + P * c: 512 * h + P * c + P], ident[:])
-                nc.scalar.copy(
-                    out=xg_f[:, 2 * h: 2 * h + 2, :, :],
-                    in_=bank[:].rearrange("p (g u r) -> p g r u", g=2, u=2),
-                )
-            xq = xqp.tile([P, 512], U32, name="xq", align_bytes=64)
-            xs = xqp.tile([P, 512], U8, name="xs", align_bytes=64)
-            nc.vector.quantize_mx(out=xq[:].bitcast(FP8X4), scales=xs[:], in_=xg[:])
+                nc.scalar.copy(out=xg_f[:, 2 * h: 2 * h + 2, :, :],
+                               in_=x_banks[m][h][:].rearrange("p (g u r) -> p g r u", g=2, u=2))
+            x_g[m] = xg
 
-            def mx(dst, gx, gw, c0, n, start, stop):
-                nc.tensor.matmul_mx(
-                    out=dst,
-                    lhsT=xq[:, P * gx: P * gx + P].bitcast(FP8X4),
-                    lhsT_scale=xs[:, P * gx: P * gx + P],
-                    rhs=wq[gw][:, c0: c0 + n].bitcast(FP8X4),
-                    rhs_scale=ws[gw][:, c0: c0 + n],
-                    start=start,
-                    stop=stop,
-                )
+        def xquant(m):
+            q = xqp.tile([P, 512], U32, name="xq", align_bytes=64)
+            s = xqp.tile([P, 512], U8, name="xs", align_bytes=64)
+            nc.vector.quantize_mx(out=q[:].bitcast(FP8X4), scales=s[:], in_=x_g[m][:])
+            x_q[m] = (q, s)
 
-            ot = op.tile([P, OUT_F], F32, name="ot")
+        def mx(m, dst, gx, c0, n, start, stop):
+            q, s = x_q[m]
+            nc.tensor.matmul_mx(
+                out=dst,
+                lhsT=q[:, P * gx: P * gx + P].bitcast(FP8X4),
+                lhsT_scale=s[:, P * gx: P * gx + P],
+                rhs=wq[:, WCOL * gx + c0: WCOL * gx + c0 + n].bitcast(FP8X4),
+                rhs_scale=ws[:, WCOL * gx + c0: WCOL * gx + c0 + n],
+                start=start,
+                stop=stop,
+            )
+
+        accs = {}
+
+        def mm(m, g):
+            acc = ps.tile([P, 512], F32, name=M_RING[g])
+            mx(m, acc[:, 0:128], g, 128, 128, True, g == 0)
+            if g > 0:
+                mx(m, acc[:, 0:128], g - 1, 640, 128, False, True)
+            mx(m, acc[:, 128:384], g, 256, 256, True, True)
+            mx(m, acc[:, 384:512], g, 512, 128, True, g == N_G - 1)
+            if g < N_G - 1:
+                mx(m, acc[:, 384:512], g + 1, 0, 128, False, True)
+            accs[(m, g)] = acc
+
+        outs = {}
+
+        def ev(m, g):
+            if g == 0:
+                outs[m] = op.tile([P, OUT_F], F32, name="ot")
+            ot = outs[m]
+            cols = slice(512 * g, 512 * g + 512)
+            if (m, g) in VIA_SCALAR:
+                nc.scalar.copy(out=ot[:, cols], in_=accs[(m, g)][:])
+                nc.gpsimd.tensor_tensor(out=ot[:, cols], in0=ot[:, cols], in1=bias[:, cols], op=ADD)
+            else:
+                nc.vector.tensor_tensor(out=ot[:, cols], in0=accs[(m, g)][:], in1=bias[:, cols], op=ADD)
+
+        def store(m, c0, c1):
+            nc.sync.dma_start(out=out[P * m: P * m + P, c0:c1], in_=outs[m][:, c0:c1])
+
+        w_t(0)
+        w_c(0)
+        xt(0)
+        w_q(0)
+        xc(0)
+        w_t(1)
+        w_c(1)
+        xquant(0)
+        w_q(1)
+        xt(1)
+        xc(1)
+        w_t(2)
+        w_c(2)
+        mm(0, 0)
+        w_q(2)
+        ev(0, 0)
+        xquant(1)
+        w_t(3)
+        w_c(3)
+        mm(0, 1)
+        w_q(3)
+        ev(0, 1)
+        xt(2)
+        xc(2)
+        mm(0, 2)
+        mm(0, 3)
+        store(0, 0, 1024)
+        ev(0, 2)
+        ev(0, 3)
+        xquant(2)
+        store(0, 1024, 2048)
+
+        for m in range(1, N_M):
+            if m + 2 < N_M:
+                xt(m + 2)
+                xc(m + 2)
             for g in range(N_G):
-                acc = po.tile([P, 512], F32, name="acc")
-                mx(acc[:, 0:128], g, g, 128, 128, True, g == 0)
-                if g > 0:
-                    mx(acc[:, 0:128], g - 1, g - 1, 640, 128, False, True)
-                mx(acc[:, 128:384], g, g, 256, 256, True, True)
-                mx(acc[:, 384:512], g, g, 512, 128, True, g == N_G - 1)
-                if g < N_G - 1:
-                    mx(acc[:, 384:512], g + 1, g + 1, 0, 128, False, True)
-                nc.vector.tensor_tensor(
-                    out=ot[:, 512 * g: 512 * g + 512], in0=acc[:], in1=bias[:, 512 * g: 512 * g + 512], op=ADD
-                )
-            nc.sync.dma_start(out=out[P * m: P * m + P, :], in_=ot[:])
+                mm(m, g)
+            for g in range(N_G):
+                ev(m, g)
+            if m + 2 < N_M:
+                xquant(m + 2)
+            if m < N_M - 1:
+                store(m, 0, OUT_F)
+            else:
+                for g in range(N_G):
+                    store(m, 512 * g, 512 * g + 512)

@@ -23,6 +23,7 @@ FLOPS = 2 * BATCH * OUT_F * WIN
 BYTES = BATCH * IN_F * 2 + OUT_F * WIN * 2 + OUT_F * 2 + BATCH * OUT_F * 4
 
 VIA_SCALAR = [(m, 0) for m in range(1, N_M)]
+X_ON_VECTOR = [(0, 0), (0, 1)]
 M_RING = ["k3", "k4", "k7", "k0"]
 X_RING = ["k5", "k6", "k1", "k2"]
 
@@ -37,8 +38,8 @@ def tile_locallayer_kernel(tc, x, W, b, mask, out):
          tc.psum_pool(name="ps", bufs=1) as ps, \
          tc.manual_schedule():
 
-        w_sb = const.tile([P, 17 * 512], BF16)
-        w_f = w_sb[:].bitcast(F32)
+        w_half = [const.tile([P, 9 * 512], BF16, name="w_sb%d" % i) for i in range(2)]
+        w_f = [t[:].bitcast(F32) for t in w_half]
         wg = const.tile([P, N_G * WCOL * 4], BF16, align_bytes=64)
         wg_f = wg[:].bitcast(F32).rearrange("p (o u) -> p o u", u=2)
         wq = const.tile([P, N_G * WCOL], U32, align_bytes=64)
@@ -49,8 +50,17 @@ def tile_locallayer_kernel(tc, x, W, b, mask, out):
         bias = const.tile([P, OUT_F], BF16)
         ident = const.tile([P, P], F32)
 
-        nc.vector.memset(brow[:].bitcast(F32), 0.0)
-        nc.sync.dma_start(out=brow[0:1, :], in_=b.unsqueeze(0))
+        nc.gpsimd.memset(brow[:].bitcast(F32), 0.0)
+        make_identity(nc, ident[:])
+        nc.gpsimd.memset(ones[:], 1.0)
+        nc.gpsimd.memset(zero[:], 0.0)
+        for i in range(2):
+            nc.vector.memset(w_f[i].rearrange("p (i w) -> p i w", w=256)[:, :, 0:168], 0.0)
+        nc.vector.memset(
+            wq[:].bitcast(I32)[:, 704: 704 + 3 * WCOL].rearrange("p (g c) -> p g c", c=WCOL)[:, :, 0:128], 0)
+        nc.vector.memset(
+            ws[:].bitcast(I32)[:, 176: 176 + 3 * 192].rearrange("p (g c) -> p g c", c=192)[:, :, 0:32], 0)
+
         w_flat = W.rearrange("a b -> (a b)")
         pitch = P * IN_F + P
 
@@ -58,7 +68,8 @@ def tile_locallayer_kernel(tc, x, W, b, mask, out):
             src = w_flat[first * pitch - 32: first * pitch - 32 + n * pitch]
             src = src.rearrange("(i l) -> i l", l=pitch)[:, 0: P * IN_F]
             src = src.rearrange("i (p q) -> p i q", q=IN_F)[:, :, 0:176]
-            dst = w_sb[:, 512 * first + 224: 512 * first + 224 + 512 * n]
+            c0 = 512 * (first % 8) + 336
+            dst = w_half[first // 8][:, c0: c0 + 512 * n]
             dst = dst.rearrange("p (i c) -> p i c", c=512)[:, :, 0:176]
             nc.sync.dma_start(out=dst, in_=src)
 
@@ -69,34 +80,27 @@ def tile_locallayer_kernel(tc, x, W, b, mask, out):
             nc.sync.dma_start(out=t[:], in_=x[P * m: P * m + P, :])
             x_sb.append(t)
 
-        nc.sync.dma_start(out=w_sb[:, 256:400], in_=W[0:P, 0:144])
-        load_w(1, 6)
         load_x(0)
-        load_w(7, 8)
-        nc.sync.dma_start(out=w_sb[:, 512 * 15 + 224: 512 * 15 + 384], in_=W[15 * P: 16 * P, IN_F - 160: IN_F])
-        for m in range(1, N_M):
+        nc.sync.dma_start(out=brow[0:1, :], in_=b.unsqueeze(0))
+        nc.sync.dma_start(out=w_half[0][:, 368:512], in_=W[0:P, 0:144])
+        load_w(1, 7)
+        load_x(1)
+        load_w(8, 7)
+        nc.sync.dma_start(out=w_half[1][:, 512 * 7 + 336: 512 * 7 + 496], in_=W[15 * P: 16 * P, IN_F - 160: IN_F])
+        for m in range(2, N_M):
             load_x(m)
-
-        make_identity(nc, ident[:])
-        nc.vector.memset(ones[:], 1.0)
-        nc.vector.memset(zero[:], 0.0)
-        nc.vector.memset(w_f[:, 200: 200 + 16 * 256].rearrange("p (i w) -> p i w", w=256)[:, :, 0:168], 0.0)
-        nc.vector.memset(
-            wq[:].bitcast(I32)[:, 704: 704 + 3 * WCOL].rearrange("p (g c) -> p g c", c=WCOL)[:, :, 0:128], 0)
-        nc.vector.memset(
-            ws[:].bitcast(I32)[:, 176: 176 + 3 * 192].rearrange("p (g c) -> p g c", c=192)[:, :, 0:32], 0)
 
         for h in range(2):
             bb = ps.tile([P, 1024], BF16, name=M_RING[h])
             for i in range(2):
                 nc.tensor.matmul(out=bb[:, 512 * i: 512 * i + 512], lhsT=ones[:],
                                  rhs=brow[:, 1024 * h + 512 * i: 1024 * h + 512 * i + 512], start=True, stop=True)
-            nc.scalar.copy(out=bias[:, 1024 * h: 1024 * h + 1024], in_=bb[:])
+            (nc.scalar.copy if h == 0 else nc.vector.tensor_copy)(out=bias[:, 1024 * h: 1024 * h + 1024], in_=bb[:])
 
         def window(ob, chunk):
             j = chunk - (ob - 1) // 2
-            base = 256 * ob + 64 * (ob % 2) + P * j
-            return w_f[:, base: base + P]
+            base = 256 * (ob % 8) + 56 + 64 * (ob % 2) + P * j
+            return w_f[ob // 8][:, base: base + P]
 
         bank_a = ps.tile([P, 512], F32, name="k0")
         bank_b = ps.tile([P, 512], F32, name="k1")
@@ -157,8 +161,9 @@ def tile_locallayer_kernel(tc, x, W, b, mask, out):
             xg = xgp.tile([P, IN_F], BF16, name="xg", align_bytes=64)
             xg_f = xg[:].bitcast(F32).rearrange("p (g r u) -> p g r u", g=N_G, u=2)
             for h in range(2):
-                nc.scalar.copy(out=xg_f[:, 2 * h: 2 * h + 2, :, :],
-                               in_=x_banks[m][h][:].rearrange("p (g u r) -> p g r u", g=2, u=2))
+                eng_copy = nc.vector.tensor_copy if (m, h) in X_ON_VECTOR else nc.scalar.copy
+                eng_copy(out=xg_f[:, 2 * h: 2 * h + 2, :, :],
+                         in_=x_banks[m][h][:].rearrange("p (g u r) -> p g r u", g=2, u=2))
             x_g[m] = xg
 
         def xquant(m):
@@ -208,14 +213,14 @@ def tile_locallayer_kernel(tc, x, W, b, mask, out):
         def store(m, c0, c1):
             nc.sync.dma_start(out=out[P * m: P * m + P, c0:c1], in_=outs[m][:, c0:c1])
 
+        xt(0)
+        xc(0)
         w_t(0)
         w_c(0)
-        xt(0)
+        xquant(0)
         w_q(0)
-        xc(0)
         w_t(1)
         w_c(1)
-        xquant(0)
         w_q(1)
         xt(1)
         xc(1)

@@ -23,6 +23,7 @@ FLOPS = 2 * BATCH * OUT_F * WIN
 BYTES = BATCH * IN_F * 2 + OUT_F * WIN * 2 + OUT_F * 2 + BATCH * OUT_F * 4
 
 VIA_SCALAR = [(m, 0) for m in range(1, N_M)]
+
 X_ON_VECTOR = [(0, 0), (0, 1)]
 M_RING = ["k3", "k4", "k7", "k0"]
 X_RING = ["k5", "k6", "k1", "k2"]
@@ -32,8 +33,8 @@ def tile_locallayer_kernel(tc, x, W, b, mask, out):
     nc = tc.nc
     with tc.tile_pool(name="const", bufs=1) as const, \
          tc.tile_pool(name="xin", bufs=N_M) as xin, \
-         tc.tile_pool(name="xgp", bufs=3) as xgp, \
-         tc.tile_pool(name="xqp", bufs=4) as xqp, \
+         tc.tile_pool(name="xgp", bufs=4) as xgp, \
+         tc.tile_pool(name="xqp", bufs=5) as xqp, \
          tc.tile_pool(name="op", bufs=4) as op, \
          tc.psum_pool(name="ps", bufs=1) as ps, \
          tc.manual_schedule():
@@ -90,12 +91,12 @@ def tile_locallayer_kernel(tc, x, W, b, mask, out):
         for m in range(2, N_M):
             load_x(m)
 
-        for h in range(2):
+        def bias_half(h):
             bb = ps.tile([P, 1024], BF16, name=M_RING[h])
             for i in range(2):
                 nc.tensor.matmul(out=bb[:, 512 * i: 512 * i + 512], lhsT=ones[:],
                                  rhs=brow[:, 1024 * h + 512 * i: 1024 * h + 512 * i + 512], start=True, stop=True)
-            (nc.scalar.copy if h == 0 else nc.vector.tensor_copy)(out=bias[:, 1024 * h: 1024 * h + 1024], in_=bb[:])
+            (nc.vector.tensor_copy if h == 1 else nc.scalar.copy)(out=bias[:, 1024 * h: 1024 * h + 1024], in_=bb[:])
 
         def window(ob, chunk):
             j = chunk - (ob - 1) // 2
@@ -105,9 +106,10 @@ def tile_locallayer_kernel(tc, x, W, b, mask, out):
         bank_a = ps.tile([P, 512], F32, name="k0")
         bank_b = ps.tile([P, 512], F32, name="k1")
         bank_c = ps.tile([P, 512], F32, name="k2")
-        for i in range(2):
-            nc.tensor.transpose(bank_a[:, 256 + P * i: 256 + P * i + P], zero[:], ident[:])
-            nc.tensor.transpose(bank_c[:, P * i: P * i + P], zero[:], ident[:])
+        def zero_planes():
+            for i in range(2):
+                nc.tensor.transpose(bank_a[:, 256 + P * i: 256 + P * i + P], zero[:], ident[:])
+                nc.tensor.transpose(bank_c[:, P * i: P * i + P], zero[:], ident[:])
 
         def quant_w(g, c0, c1):
             lo = WCOL * g + c0
@@ -152,7 +154,7 @@ def tile_locallayer_kernel(tc, x, W, b, mask, out):
             x_f = x_sb[m][:].bitcast(F32)
             x_banks[m] = []
             for h in range(2):
-                bank = ps.tile([P, 512], F32, name=X_RING[h + (2 if (m % 2 == 0 and m >= 2) else 0)])
+                bank = ps.tile([P, 512], F32, name=X_RING[h + (2 if (m % 2 == 1 and m >= 3) else 0)])
                 for c in range(4):
                     nc.tensor.transpose(bank[:, P * c: P * c + P], x_f[:, 512 * h + P * c: 512 * h + P * c + P], ident[:])
                 x_banks[m].append(bank)
@@ -215,6 +217,9 @@ def tile_locallayer_kernel(tc, x, W, b, mask, out):
 
         xt(0)
         xc(0)
+        bias_half(0)
+        bias_half(1)
+        zero_planes()
         w_t(0)
         w_c(0)
         xquant(0)
@@ -228,15 +233,16 @@ def tile_locallayer_kernel(tc, x, W, b, mask, out):
         w_c(2)
         mm(0, 0)
         w_q(2)
-        ev(0, 0)
-        xquant(1)
+        xt(2)
         w_t(3)
         w_c(3)
         mm(0, 1)
         w_q(3)
+        ev(0, 0)
+        xquant(1)
         ev(0, 1)
-        xt(2)
         xc(2)
+        xt(3)
         mm(0, 2)
         mm(0, 3)
         store(0, 0, 1024)
@@ -245,18 +251,19 @@ def tile_locallayer_kernel(tc, x, W, b, mask, out):
         xquant(2)
         store(0, 1024, 2048)
 
+        xc(3)
         for m in range(1, N_M):
-            if m + 2 < N_M:
-                xt(m + 2)
-                xc(m + 2)
+            if m + 3 < N_M:
+                xt(m + 3)
             for g in range(N_G):
                 mm(m, g)
-            for g in range(N_G):
-                ev(m, g)
+            ev(m, 0)
+            if m + 3 < N_M:
+                xc(m + 3)
+            ev(m, 1)
+            store(m, 0, 1024)
+            ev(m, 2)
+            ev(m, 3)
             if m + 2 < N_M:
                 xquant(m + 2)
-            if m < N_M - 1:
-                store(m, 0, OUT_F)
-            else:
-                for g in range(N_G):
-                    store(m, 512 * g, 512 * g + 512)
+            store(m, 1024, 2048)

@@ -17,16 +17,24 @@ WIN = 64
 N_M = BATCH // P
 N_G = IN_F // 512
 N_OB = OUT_F // P
-WCOL = 768
+SHIFT = 16
+WCOL = 640
+SLOT = 192
+PAD = 104
 
 FLOPS = 2 * BATCH * OUT_F * WIN
 BYTES = BATCH * IN_F * 2 + OUT_F * WIN * 2 + OUT_F * 2 + BATCH * OUT_F * 4
 
+HALO = 48
+
 VIA_SCALAR = [(m, 0) for m in range(1, N_M)]
 
-X_ON_VECTOR = [(0, 0), (0, 1)]
-M_RING = ["k3", "k4", "k7", "k0"]
-X_RING = ["k5", "k6", "k1", "k2"]
+X_ON_VECTOR = [(0, 1)]
+W_BANKS = [("k0", "k1"), ("k2", "k3")]
+HALO_ORDER = [3, 0, 1, 2]
+BIAS_BANKS = ["k7", "k5"]
+M_RING = ["k6", "k0", "k1", "k2"]
+X_RING = [("k5", "k7"), ("k3", "k4")]
 
 
 def tile_locallayer_kernel(tc, x, W, b, mask, out):
@@ -36,42 +44,49 @@ def tile_locallayer_kernel(tc, x, W, b, mask, out):
          tc.tile_pool(name="xgp", bufs=4) as xgp, \
          tc.tile_pool(name="xqp", bufs=5) as xqp, \
          tc.tile_pool(name="op", bufs=4) as op, \
+         tc.tile_pool(name="stp", bufs=2) as stp, \
          tc.psum_pool(name="ps", bufs=1) as ps, \
          tc.manual_schedule():
 
-        w_half = [const.tile([P, 9 * 512], BF16, name="w_sb%d" % i) for i in range(2)]
-        w_f = [t[:].bitcast(F32) for t in w_half]
+        w_sb = [const.tile([P, n * 2 * SLOT], BF16, name="w_sb%d" % i) for i, n in enumerate((6, 5, 8))]
+        w_f = [t[:].bitcast(F32) for t in w_sb]
         wg = const.tile([P, N_G * WCOL * 4], BF16, align_bytes=64)
         wg_f = wg[:].bitcast(F32).rearrange("p (o u) -> p o u", u=2)
         wq = const.tile([P, N_G * WCOL], U32, align_bytes=64)
         ws = const.tile([P, N_G * WCOL], U8, align_bytes=64)
-        zero = const.tile([P, P], F32)
+        zero = const.tile([P, 512], BF16)
         ones = const.tile([P, P], BF16)
         brow = const.tile([P, OUT_F], BF16)
         bias = const.tile([P, OUT_F], BF16)
         ident = const.tile([P, P], F32)
 
-        nc.gpsimd.memset(brow[:].bitcast(F32), 0.0)
-        make_identity(nc, ident[:])
+        nc.vector.memset(brow[:].bitcast(F32), 0.0)
+        nc.gpsimd.memset(w_f[0].rearrange("p (i w) -> p i w", w=SLOT)[:, :, 0:PAD], 0.0)
+        nc.vector.memset(zero[:].bitcast(F32), 0.0)
         nc.gpsimd.memset(ones[:], 1.0)
-        nc.gpsimd.memset(zero[:], 0.0)
-        for i in range(2):
-            nc.vector.memset(w_f[i].rearrange("p (i w) -> p i w", w=256)[:, :, 0:168], 0.0)
-        nc.vector.memset(
-            wq[:].bitcast(I32)[:, 704: 704 + 3 * WCOL].rearrange("p (g c) -> p g c", c=WCOL)[:, :, 0:128], 0)
-        nc.vector.memset(
-            ws[:].bitcast(I32)[:, 176: 176 + 3 * 192].rearrange("p (g c) -> p g c", c=192)[:, :, 0:32], 0)
+        make_identity(nc, ident[:])
+        for i in (1, 2):
+            nc.vector.memset(w_f[i].rearrange("p (i w) -> p i w", w=SLOT)[:, :, 0:PAD], 0.0)
+        nc.vector.memset(w_f[2][:, 7 * SLOT + PAD: 7 * SLOT + P], 0.0)
+        nc.gpsimd.memset(wg_f.rearrange("p (g c) u -> p g c u", c=WCOL)[:, :, 512 + HALO: 576, :], 0.0)
+        nc.gpsimd.memset(wq[:].bitcast(I32).rearrange("p (g c) -> p g c", c=WCOL)[:, :, 576:640], 0)
+        nc.gpsimd.memset(ws[:].bitcast(I32).rearrange("p (g c) -> p g c", c=WCOL // 4)[:, :, 144:160], 0)
 
         w_flat = W.rearrange("a b -> (a b)")
         pitch = P * IN_F + P
 
+        def w_place(ob):
+            i = 0 if ob < 5 else 1 if ob < 9 else 2
+            return i, SLOT * (ob - (0, 5, 9)[i])
+
         def load_w(first, n):
-            src = w_flat[first * pitch - 32: first * pitch - 32 + n * pitch]
+            i, lo = w_place(first)
+            start = first * pitch - SHIFT * IN_F - 48
+            src = w_flat[start: start + n * pitch]
             src = src.rearrange("(i l) -> i l", l=pitch)[:, 0: P * IN_F]
             src = src.rearrange("i (p q) -> p i q", q=IN_F)[:, :, 0:176]
-            c0 = 512 * (first % 8) + 336
-            dst = w_half[first // 8][:, c0: c0 + 512 * n]
-            dst = dst.rearrange("p (i c) -> p i c", c=512)[:, :, 0:176]
+            dst = w_sb[i][:, 2 * lo: 2 * lo + 2 * SLOT * n]
+            dst = dst.rearrange("p (i c) -> p i c", c=2 * SLOT)[:, :, 2 * PAD: 2 * SLOT]
             nc.sync.dma_start(out=dst, in_=src)
 
         x_sb = []
@@ -83,68 +98,76 @@ def tile_locallayer_kernel(tc, x, W, b, mask, out):
 
         load_x(0)
         nc.sync.dma_start(out=brow[0:1, :], in_=b.unsqueeze(0))
-        nc.sync.dma_start(out=w_half[0][:, 368:512], in_=W[0:P, 0:144])
-        load_w(1, 7)
-        load_x(1)
-        load_w(8, 7)
-        nc.sync.dma_start(out=w_half[1][:, 512 * 7 + 336: 512 * 7 + 496], in_=W[15 * P: 16 * P, IN_F - 160: IN_F])
-        for m in range(2, N_M):
+        nc.sync.dma_start(out=w_sb[0][:, 2 * P: 2 * SLOT], in_=W[0:P, 0:P])
+        load_w(1, 4)
+        c16 = 2 * (7 * SLOT + PAD)
+        nc.sync.dma_start(out=w_sb[2][0:SHIFT, c16: c16 + 48], in_=W[OUT_F - SHIFT: OUT_F, IN_F - 48: IN_F])
+        load_w(5, 4)
+        load_w(9, 7)
+        for m in range(1, N_M):
             load_x(m)
 
-        def bias_half(h):
-            bb = ps.tile([P, 1024], BF16, name=M_RING[h])
+        bias_banks = {}
+
+        def bias_mm(h):
+            bank = ps.tile([P, 1024], BF16, name=BIAS_BANKS[h])
             for i in range(2):
-                nc.tensor.matmul(out=bb[:, 512 * i: 512 * i + 512], lhsT=ones[:],
+                nc.tensor.matmul(out=bank[:, 512 * i: 512 * i + 512], lhsT=ones[:],
                                  rhs=brow[:, 1024 * h + 512 * i: 1024 * h + 512 * i + 512], start=True, stop=True)
-            (nc.vector.tensor_copy if h == 1 else nc.scalar.copy)(out=bias[:, 1024 * h: 1024 * h + 1024], in_=bb[:])
+            bias_banks[h] = bank
+
+        def bias_copy(h, eng_copy):
+            eng_copy(out=bias[:, 1024 * h: 1024 * h + 1024], in_=bias_banks[h][:])
 
         def window(ob, chunk):
-            j = chunk - (ob - 1) // 2
-            base = 256 * (ob % 8) + 56 + 64 * (ob % 2) + P * j
-            return w_f[ob // 8][:, base: base + P]
+            i, lo = w_place(ob)
+            lo += PAD + P * chunk - 64 * ob + 24
+            return w_f[i][:, lo: lo + P]
 
-        bank_a = ps.tile([P, 512], F32, name="k0")
-        bank_b = ps.tile([P, 512], F32, name="k1")
-        bank_c = ps.tile([P, 512], F32, name="k2")
-        def zero_planes():
-            for i in range(2):
-                nc.tensor.transpose(bank_a[:, 256 + P * i: 256 + P * i + P], zero[:], ident[:])
-                nc.tensor.transpose(bank_c[:, P * i: P * i + P], zero[:], ident[:])
+        w_banks = [[ps.tile([P, 512], F32, name=k) for k in pair] for pair in W_BANKS]
+        bank_c = ps.tile([P, 512], F32, name="k4")
+        for bank in w_banks[0] + w_banks[1] + [bank_c]:
+            nc.tensor.matmul(out=bank[:], lhsT=zero[:, 0:P], rhs=zero[:], start=True, stop=True)
 
         def quant_w(g, c0, c1):
             lo = WCOL * g + c0
             hi = WCOL * g + c1
             nc.vector.quantize_mx(out=wq[:, lo:hi].bitcast(FP8X4), scales=ws[:, lo:hi], in_=wg[:, 4 * lo: 4 * hi])
 
-        def w_copy(eng_copy, g, bank, col0, lo, hi):
-            eng_copy(out=wg_f[:, WCOL * g + col0 + lo: WCOL * g + col0 + hi, :],
-                     in_=bank[:].rearrange("p (u o) -> p o u", u=2)[:, lo:hi, :])
+        def w_copy(eng_copy, g, src, lo, col0, n):
+            eng_copy(out=wg_f[:, WCOL * g + col0: WCOL * g + col0 + n, :],
+                     in_=src.rearrange("p (u o) -> p o u", u=2)[:, lo: lo + n, :])
 
         def w_t(g):
-            if g > 0:
-                nc.tensor.transpose(bank_a[:, 0:P], window(4 * g - 1, 2 * g), ident[:])
-            nc.tensor.transpose(bank_a[:, P:256], window(4 * g, 2 * g), ident[:])
-            for u in range(2):
-                for i in range(2):
-                    nc.tensor.transpose(bank_b[:, 256 * u + P * i: 256 * u + P * i + P],
-                                        window(4 * g + 1 + i, 2 * g + u), ident[:])
-            nc.tensor.transpose(bank_c[:, 256:384], window(4 * g + 3, 2 * g + 1), ident[:])
-            if g < N_G - 1:
-                nc.tensor.transpose(bank_c[:, 384:512], window(4 * g + 4, 2 * g + 1), ident[:])
+            bank_a, bank_b = w_banks[g % 2]
+            lo = SHIFT if g == 0 else 0
+            nc.tensor.transpose(bank_a[:, lo: lo + P], window(4 * g, 2 * g), ident[:])
+            nc.tensor.transpose(bank_a[:, P:256], window(4 * g + 1, 2 * g), ident[:])
+            nc.tensor.transpose(bank_b[:, 0:P], window(4 * g + 2, 2 * g), ident[:])
+            nc.tensor.transpose(bank_b[:, 256:384], window(4 * g + 2, 2 * g + 1), ident[:])
+            nc.tensor.transpose(bank_b[:, 384:512], window(4 * g + 3, 2 * g + 1), ident[:])
 
-        def w_c(g):
-            w_copy(nc.scalar.copy, g, bank_a, 0, 64 if g > 0 else 128, 256)
-            w_copy(nc.vector.tensor_copy, g, bank_c, 512, 0, 192 if g < N_G - 1 else 128)
-            w_copy(nc.scalar.copy, g, bank_b, 256, 0, 256)
+        def w_h(g):
+            c = (N_G + HALO_ORDER.index(g)) * HALO
+            nc.tensor.transpose(bank_c[:, c: c + P], window(4 * g + 4, 2 * g + 1), ident[:])
 
-        def w_q(g):
-            if g > 0:
-                quant_w(g, 64, 128)
-            quant_w(g, 128, 256)
-            quant_w(g, 512, 640)
-            if g < N_G - 1:
-                quant_w(g, 640, 704)
+        def wa(g, eng_copy):
+            w_copy(eng_copy, g, w_banks[g % 2][0][:], 0, 0, 256)
+
+        def wb(g, eng_copy):
+            w_copy(eng_copy, g, w_banks[g % 2][1][:], 0, 256, 256)
+
+        def wc(g, eng_copy):
+            w_copy(eng_copy, g, bank_c[:, 0: 2 * N_G * HALO], HALO * HALO_ORDER.index(g), 512, HALO)
+
+        def qa(g):
+            quant_w(g, 0, 256)
+
+        def qb(g):
             quant_w(g, 256, 512)
+
+        def qc(g):
+            quant_w(g, 512, 576)
 
         x_banks = {}
         x_q = {}
@@ -154,7 +177,7 @@ def tile_locallayer_kernel(tc, x, W, b, mask, out):
             x_f = x_sb[m][:].bitcast(F32)
             x_banks[m] = []
             for h in range(2):
-                bank = ps.tile([P, 512], F32, name=X_RING[h + (2 if (m % 2 == 1 and m >= 3) else 0)])
+                bank = ps.tile([P, 512], F32, name=("k5", "k6")[h] if m == 0 else X_RING[(m - 1) % 2][h])
                 for c in range(4):
                     nc.tensor.transpose(bank[:, P * c: P * c + P], x_f[:, 512 * h + P * c: 512 * h + P * c + P], ident[:])
                 x_banks[m].append(bank)
@@ -190,80 +213,100 @@ def tile_locallayer_kernel(tc, x, W, b, mask, out):
 
         def mm(m, g):
             acc = ps.tile([P, 512], F32, name=M_RING[g])
-            mx(m, acc[:, 0:128], g, 128, 128, True, g == 0)
-            if g > 0:
-                mx(m, acc[:, 0:128], g - 1, 640, 128, False, True)
-            mx(m, acc[:, 128:384], g, 256, 256, True, True)
-            mx(m, acc[:, 384:512], g, 512, 128, True, g == N_G - 1)
-            if g < N_G - 1:
-                mx(m, acc[:, 384:512], g + 1, 0, 128, False, True)
+            mx(m, acc[:], g, 0, 512, True, False)
+            mx(m, acc[:, 0:P], (g - 1) % N_G, 512, P, False, True)
             accs[(m, g)] = acc
 
         outs = {}
 
         def ev(m, g):
-            if g == 0:
+            if m not in outs:
                 outs[m] = op.tile([P, OUT_F], F32, name="ot")
             ot = outs[m]
-            cols = slice(512 * g, 512 * g + 512)
-            if (m, g) in VIA_SCALAR:
-                nc.scalar.copy(out=ot[:, cols], in_=accs[(m, g)][:])
-                nc.gpsimd.tensor_tensor(out=ot[:, cols], in0=ot[:, cols], in1=bias[:, cols], op=ADD)
+            acc = accs[(m, g)]
+            if g == 0:
+                parts = [(SHIFT, 512, 0), (0, SHIFT, OUT_F - SHIFT)]
             else:
-                nc.vector.tensor_tensor(out=ot[:, cols], in0=accs[(m, g)][:], in1=bias[:, cols], op=ADD)
+                parts = [(0, 512, 512 * g - SHIFT)]
+            src = acc
+            if (m, g) in VIA_SCALAR:
+                src = stp.tile([P, 512], F32, name="st")
+                nc.scalar.copy(out=src[:], in_=acc[:])
+            add = nc.gpsimd.tensor_tensor if (m, g) in VIA_SCALAR else nc.vector.tensor_tensor
+            for lo, hi, c in parts:
+                add(out=ot[:, c: c + hi - lo], in0=src[:, lo:hi], in1=bias[:, c: c + hi - lo], op=ADD)
 
         def store(m, c0, c1):
             nc.sync.dma_start(out=out[P * m: P * m + P, c0:c1], in_=outs[m][:, c0:c1])
 
         xt(0)
         xc(0)
-        bias_half(0)
-        bias_half(1)
-        zero_planes()
         w_t(0)
-        w_c(0)
-        xquant(0)
-        w_q(0)
+        w_h(3)
+        w_h(0)
         w_t(1)
-        w_c(1)
-        w_q(1)
-        xt(1)
-        xc(1)
+        w_h(1)
+        bias_mm(0)
+        bias_mm(1)
+        wa(0, nc.scalar.copy)
+        wb(0, nc.scalar.copy)
+        xquant(0)
+        wc(3, nc.vector.tensor_copy)
+        wc(0, nc.vector.tensor_copy)
+        qa(0)
+        qc(3)
+        wa(1, nc.vector.tensor_copy)
+        qb(0)
+        wb(1, nc.scalar.copy)
         w_t(2)
-        w_c(2)
+        w_h(2)
+        bias_copy(0, nc.scalar.copy)
+        wa(2, nc.scalar.copy)
         mm(0, 0)
-        w_q(2)
-        xt(2)
         w_t(3)
-        w_c(3)
+        qc(0)
+        qa(1)
+        wc(1, nc.vector.tensor_copy)
+        qb(1)
         mm(0, 1)
-        w_q(3)
+        bias_copy(1, nc.vector.tensor_copy)
+        wb(2, nc.scalar.copy)
+        wa(3, nc.scalar.copy)
+        wc(2, nc.vector.tensor_copy)
+        qc(1)
+        qa(2)
+        xt(1)
         ev(0, 0)
-        xquant(1)
-        ev(0, 1)
-        xc(2)
-        xt(3)
+        qb(2)
+        qc(2)
         mm(0, 2)
+        wb(3, nc.scalar.copy)
+        xt(2)
+        xc(1)
+        ev(0, 1)
+        qa(3)
+        qb(3)
         mm(0, 3)
-        store(0, 0, 1024)
+        store(0, 0, 960)
+        xquant(1)
+        xc(2)
         ev(0, 2)
         ev(0, 3)
-        xquant(2)
-        store(0, 1024, 2048)
+        store(0, 960, 2048)
 
-        xc(3)
         for m in range(1, N_M):
-            if m + 3 < N_M:
-                xt(m + 3)
+            if m + 1 < N_M:
+                xquant(m + 1)
             for g in range(N_G):
                 mm(m, g)
             ev(m, 0)
-            if m + 3 < N_M:
-                xc(m + 3)
             ev(m, 1)
-            store(m, 0, 1024)
+            for i in (m + 2, m + 3):
+                if m % 2 == 1 and i < N_M:
+                    xt(i)
+            if m + 2 < N_M:
+                xc(m + 2)
+            store(m, 0, 960)
             ev(m, 2)
             ev(m, 3)
-            if m + 2 < N_M:
-                xquant(m + 2)
-            store(m, 1024, 2048)
+            store(m, 960, 2048)

@@ -27,14 +27,14 @@ BYTES = BATCH * IN_F * 2 + OUT_F * WIN * 2 + OUT_F * 2 + BATCH * OUT_F * 4
 
 HALO = 48
 
-VIA_SCALAR = [(m, 0) for m in range(1, N_M)]
+GP_COLS = {(m, 0): 512 for m in range(1, N_M)}
 
 X_ON_VECTOR = [(0, 1)]
 W_BANKS = [("k0", "k1"), ("k2", "k3")]
 HALO_ORDER = [3, 0, 1, 2]
 BIAS_BANKS = ["k7", "k5"]
-M_RING = ["k6", "k0", "k1", "k2"]
-X_RING = [("k5", "k7"), ("k3", "k4")]
+M_RING = ["k6", "k0", "k1", "k2", "k3", "k4"]
+X_BANKS = {0: ("k5", "k6"), 2: ("k3", "k4")}
 
 
 def tile_locallayer_kernel(tc, x, W, b, mask, out):
@@ -166,6 +166,9 @@ def tile_locallayer_kernel(tc, x, W, b, mask, out):
         def qb(g):
             quant_w(g, 256, 512)
 
+        def qab(g):
+            quant_w(g, 0, 512)
+
         def qc(g):
             quant_w(g, 512, 576)
 
@@ -177,7 +180,7 @@ def tile_locallayer_kernel(tc, x, W, b, mask, out):
             x_f = x_sb[m][:].bitcast(F32)
             x_banks[m] = []
             for h in range(2):
-                bank = ps.tile([P, 512], F32, name=("k5", "k6")[h] if m == 0 else X_RING[(m - 1) % 2][h])
+                bank = ps.tile([P, 512], F32, name=X_BANKS.get(m, ("k5", "k7"))[h])
                 for c in range(4):
                     nc.tensor.transpose(bank[:, P * c: P * c + P], x_f[:, 512 * h + P * c: 512 * h + P * c + P], ident[:])
                 x_banks[m].append(bank)
@@ -212,7 +215,7 @@ def tile_locallayer_kernel(tc, x, W, b, mask, out):
         accs = {}
 
         def mm(m, g):
-            acc = ps.tile([P, 512], F32, name=M_RING[g])
+            acc = ps.tile([P, 512], F32, name=M_RING[(N_G * m + g) % len(M_RING)])
             mx(m, acc[:], g, 0, 512, True, False)
             mx(m, acc[:, 0:P], (g - 1) % N_G, 512, P, False, True)
             accs[(m, g)] = acc
@@ -224,17 +227,22 @@ def tile_locallayer_kernel(tc, x, W, b, mask, out):
                 outs[m] = op.tile([P, OUT_F], F32, name="ot")
             ot = outs[m]
             acc = accs[(m, g)]
-            if g == 0:
-                parts = [(SHIFT, 512, 0), (0, SHIFT, OUT_F - SHIFT)]
-            else:
-                parts = [(0, 512, 512 * g - SHIFT)]
-            src = acc
-            if (m, g) in VIA_SCALAR:
-                src = stp.tile([P, 512], F32, name="st")
-                nc.scalar.copy(out=src[:], in_=acc[:])
-            add = nc.gpsimd.tensor_tensor if (m, g) in VIA_SCALAR else nc.vector.tensor_tensor
-            for lo, hi, c in parts:
-                add(out=ot[:, c: c + hi - lo], in0=src[:, lo:hi], in1=bias[:, c: c + hi - lo], op=ADD)
+            n = GP_COLS.get((m, g), 0)
+
+            def add_bias(add, src, lo, hi):
+                for a, z, c in ((0, SHIFT, OUT_F - SHIFT), (SHIFT, 512, 0)) if g == 0 else ((0, 512, 512 * g - SHIFT),):
+                    a = max(a, lo)
+                    z = min(z, hi)
+                    if a < z:
+                        d = c + a - (SHIFT if g == 0 and a >= SHIFT else 0)
+                        add(out=ot[:, d: d + z - a], in0=src[:, a:z], in1=bias[:, d: d + z - a], op=ADD)
+
+            if n > 0:
+                st = stp.tile([P, n], F32, name="st%d" % n)
+                nc.scalar.copy(out=st[:], in_=acc[:, 0:n])
+                add_bias(nc.gpsimd.tensor_tensor, st, 0, n)
+            if n < 512:
+                add_bias(nc.vector.tensor_tensor, acc, n, 512)
 
         def store(m, c0, c1):
             nc.sync.dma_start(out=out[P * m: P * m + P, c0:c1], in_=outs[m][:, c0:c1])
@@ -261,31 +269,28 @@ def tile_locallayer_kernel(tc, x, W, b, mask, out):
         w_t(2)
         w_h(2)
         bias_copy(0, nc.scalar.copy)
+        bias_copy(1, nc.scalar.copy)
         wa(2, nc.scalar.copy)
         mm(0, 0)
         w_t(3)
         qc(0)
-        qa(1)
         wc(1, nc.vector.tensor_copy)
-        qb(1)
+        qab(1)
         mm(0, 1)
-        bias_copy(1, nc.vector.tensor_copy)
         wb(2, nc.scalar.copy)
         wa(3, nc.scalar.copy)
         wc(2, nc.vector.tensor_copy)
         qc(1)
-        qa(2)
         xt(1)
         ev(0, 0)
-        qb(2)
+        qab(2)
         qc(2)
         mm(0, 2)
         wb(3, nc.scalar.copy)
         xt(2)
         xc(1)
         ev(0, 1)
-        qa(3)
-        qb(3)
+        qab(3)
         mm(0, 3)
         store(0, 0, 960)
         xquant(1)
@@ -301,9 +306,8 @@ def tile_locallayer_kernel(tc, x, W, b, mask, out):
                 mm(m, g)
             ev(m, 0)
             ev(m, 1)
-            for i in (m + 2, m + 3):
-                if m % 2 == 1 and i < N_M:
-                    xt(i)
+            if m + 2 < N_M:
+                xt(m + 2)
             if m + 2 < N_M:
                 xc(m + 2)
             store(m, 0, 960)

import concourse.mybir as mybir
from concourse.masks import make_identity

F32 = mybir.dt.float32
I32 = mybir.dt.int32
BF16 = mybir.dt.bfloat16
U32 = mybir.dt.uint32
U8 = mybir.dt.uint8
FP8X4 = mybir.dt.float8_e4m3fn_x4
ADD = mybir.AluOpType.add

P = 128
BATCH = 1024
IN_F = 2048
OUT_F = 2048
WIN = 64
N_M = BATCH // P
N_G = IN_F // 512
N_OB = OUT_F // P
SHIFT = 16
WCOL = 640
SLOT = 192
PAD = 104

FLOPS = 2 * BATCH * OUT_F * WIN
BYTES = BATCH * IN_F * 2 + OUT_F * WIN * 2 + OUT_F * 2 + BATCH * OUT_F * 4

HALO = 48

GP_COLS = {(m, 0): 512 for m in range(1, N_M)}

X_ON_VECTOR = [(0, 1)]
W_BANKS = [("k0", "k1"), ("k2", "k3")]
HALO_ORDER = [3, 0, 1, 2]
BIAS_BANKS = ["k7", "k5"]
M_RING = ["k6", "k0", "k1", "k2", "k3", "k4"]
X_BANKS = {0: ("k5", "k6"), 2: ("k3", "k4")}


def tile_locallayer_kernel(tc, x, W, b, mask, out):
    nc = tc.nc
    with tc.tile_pool(name="const", bufs=1) as const, \
         tc.tile_pool(name="xin", bufs=N_M) as xin, \
         tc.tile_pool(name="xgp", bufs=4) as xgp, \
         tc.tile_pool(name="xqp", bufs=5) as xqp, \
         tc.tile_pool(name="op", bufs=4) as op, \
         tc.tile_pool(name="stp", bufs=2) as stp, \
         tc.psum_pool(name="ps", bufs=1) as ps, \
         tc.manual_schedule():

        w_sb = [const.tile([P, n * 2 * SLOT], BF16, name="w_sb%d" % i) for i, n in enumerate((6, 5, 8))]
        w_f = [t[:].bitcast(F32) for t in w_sb]
        wg = const.tile([P, N_G * WCOL * 4], BF16, align_bytes=64)
        wg_f = wg[:].bitcast(F32).rearrange("p (o u) -> p o u", u=2)
        wq = const.tile([P, N_G * WCOL], U32, align_bytes=64)
        ws = const.tile([P, N_G * WCOL], U8, align_bytes=64)
        zero = const.tile([P, 512], BF16)
        ones = const.tile([P, P], BF16)
        brow = const.tile([P, OUT_F], BF16)
        bias = const.tile([P, OUT_F], BF16)
        ident = const.tile([P, P], F32)

        nc.vector.memset(brow[:].bitcast(F32), 0.0)
        nc.gpsimd.memset(w_f[0].rearrange("p (i w) -> p i w", w=SLOT)[:, :, 0:PAD], 0.0)
        nc.vector.memset(zero[:].bitcast(F32), 0.0)
        nc.gpsimd.memset(ones[:], 1.0)
        make_identity(nc, ident[:])
        for i in (1, 2):
            nc.vector.memset(w_f[i].rearrange("p (i w) -> p i w", w=SLOT)[:, :, 0:PAD], 0.0)
        nc.vector.memset(w_f[2][:, 7 * SLOT + PAD: 7 * SLOT + P], 0.0)
        nc.gpsimd.memset(wg_f.rearrange("p (g c) u -> p g c u", c=WCOL)[:, :, 512 + HALO: 576, :], 0.0)
        nc.gpsimd.memset(wq[:].bitcast(I32).rearrange("p (g c) -> p g c", c=WCOL)[:, :, 576:640], 0)
        nc.gpsimd.memset(ws[:].bitcast(I32).rearrange("p (g c) -> p g c", c=WCOL // 4)[:, :, 144:160], 0)

        w_flat = W.rearrange("a b -> (a b)")
        pitch = P * IN_F + P

        def w_place(ob):
            i = 0 if ob < 5 else 1 if ob < 9 else 2
            return i, SLOT * (ob - (0, 5, 9)[i])

        def load_w(first, n):
            i, lo = w_place(first)
            start = first * pitch - SHIFT * IN_F - 48
            src = w_flat[start: start + n * pitch]
            src = src.rearrange("(i l) -> i l", l=pitch)[:, 0: P * IN_F]
            src = src.rearrange("i (p q) -> p i q", q=IN_F)[:, :, 0:176]
            dst = w_sb[i][:, 2 * lo: 2 * lo + 2 * SLOT * n]
            dst = dst.rearrange("p (i c) -> p i c", c=2 * SLOT)[:, :, 2 * PAD: 2 * SLOT]
            nc.sync.dma_start(out=dst, in_=src)

        x_sb = []

        def load_x(m):
            t = xin.tile([P, IN_F], BF16, name="x_sb")
            nc.sync.dma_start(out=t[:], in_=x[P * m: P * m + P, :])
            x_sb.append(t)

        load_x(0)
        nc.sync.dma_start(out=brow[0:1, :], in_=b.unsqueeze(0))
        nc.sync.dma_start(out=w_sb[0][:, 2 * P: 2 * SLOT], in_=W[0:P, 0:P])
        load_w(1, 4)
        c16 = 2 * (7 * SLOT + PAD)
        nc.sync.dma_start(out=w_sb[2][0:SHIFT, c16: c16 + 48], in_=W[OUT_F - SHIFT: OUT_F, IN_F - 48: IN_F])
        load_w(5, 4)
        load_w(9, 7)
        for m in range(1, N_M):
            load_x(m)

        bias_banks = {}

        def bias_mm(h):
            bank = ps.tile([P, 1024], BF16, name=BIAS_BANKS[h])
            for i in range(2):
                nc.tensor.matmul(out=bank[:, 512 * i: 512 * i + 512], lhsT=ones[:],
                                 rhs=brow[:, 1024 * h + 512 * i: 1024 * h + 512 * i + 512], start=True, stop=True)
            bias_banks[h] = bank

        def bias_copy(h, eng_copy):
            eng_copy(out=bias[:, 1024 * h: 1024 * h + 1024], in_=bias_banks[h][:])

        def window(ob, chunk):
            i, lo = w_place(ob)
            lo += PAD + P * chunk - 64 * ob + 24
            return w_f[i][:, lo: lo + P]

        w_banks = [[ps.tile([P, 512], F32, name=k) for k in pair] for pair in W_BANKS]
        bank_c = ps.tile([P, 512], F32, name="k4")
        for bank in w_banks[0] + w_banks[1] + [bank_c]:
            nc.tensor.matmul(out=bank[:], lhsT=zero[:, 0:P], rhs=zero[:], start=True, stop=True)

        def quant_w(g, c0, c1):
            lo = WCOL * g + c0
            hi = WCOL * g + c1
            nc.vector.quantize_mx(out=wq[:, lo:hi].bitcast(FP8X4), scales=ws[:, lo:hi], in_=wg[:, 4 * lo: 4 * hi])

        def w_copy(eng_copy, g, src, lo, col0, n):
            eng_copy(out=wg_f[:, WCOL * g + col0: WCOL * g + col0 + n, :],
                     in_=src.rearrange("p (u o) -> p o u", u=2)[:, lo: lo + n, :])

        def w_t(g):
            bank_a, bank_b = w_banks[g % 2]
            lo = SHIFT if g == 0 else 0
            nc.tensor.transpose(bank_a[:, lo: lo + P], window(4 * g, 2 * g), ident[:])
            nc.tensor.transpose(bank_a[:, P:256], window(4 * g + 1, 2 * g), ident[:])
            nc.tensor.transpose(bank_b[:, 0:P], window(4 * g + 2, 2 * g), ident[:])
            nc.tensor.transpose(bank_b[:, 256:384], window(4 * g + 2, 2 * g + 1), ident[:])
            nc.tensor.transpose(bank_b[:, 384:512], window(4 * g + 3, 2 * g + 1), ident[:])

        def w_h(g):
            c = (N_G + HALO_ORDER.index(g)) * HALO
            nc.tensor.transpose(bank_c[:, c: c + P], window(4 * g + 4, 2 * g + 1), ident[:])

        def wa(g, eng_copy):
            w_copy(eng_copy, g, w_banks[g % 2][0][:], 0, 0, 256)

        def wb(g, eng_copy):
            w_copy(eng_copy, g, w_banks[g % 2][1][:], 0, 256, 256)

        def wc(g, eng_copy):
            w_copy(eng_copy, g, bank_c[:, 0: 2 * N_G * HALO], HALO * HALO_ORDER.index(g), 512, HALO)

        def qa(g):
            quant_w(g, 0, 256)

        def qb(g):
            quant_w(g, 256, 512)

        def qab(g):
            quant_w(g, 0, 512)

        def qc(g):
            quant_w(g, 512, 576)

        x_banks = {}
        x_q = {}
        x_g = {}

        def xt(m):
            x_f = x_sb[m][:].bitcast(F32)
            x_banks[m] = []
            for h in range(2):
                bank = ps.tile([P, 512], F32, name=X_BANKS.get(m, ("k5", "k7"))[h])
                for c in range(4):
                    nc.tensor.transpose(bank[:, P * c: P * c + P], x_f[:, 512 * h + P * c: 512 * h + P * c + P], ident[:])
                x_banks[m].append(bank)

        def xc(m):
            xg = xgp.tile([P, IN_F], BF16, name="xg", align_bytes=64)
            xg_f = xg[:].bitcast(F32).rearrange("p (g r u) -> p g r u", g=N_G, u=2)
            for h in range(2):
                eng_copy = nc.vector.tensor_copy if (m, h) in X_ON_VECTOR else nc.scalar.copy
                eng_copy(out=xg_f[:, 2 * h: 2 * h + 2, :, :],
                         in_=x_banks[m][h][:].rearrange("p (g u r) -> p g r u", g=2, u=2))
            x_g[m] = xg

        def xquant(m):
            q = xqp.tile([P, 512], U32, name="xq", align_bytes=64)
            s = xqp.tile([P, 512], U8, name="xs", align_bytes=64)
            nc.vector.quantize_mx(out=q[:].bitcast(FP8X4), scales=s[:], in_=x_g[m][:])
            x_q[m] = (q, s)

        def mx(m, dst, gx, c0, n, start, stop):
            q, s = x_q[m]
            nc.tensor.matmul_mx(
                out=dst,
                lhsT=q[:, P * gx: P * gx + P].bitcast(FP8X4),
                lhsT_scale=s[:, P * gx: P * gx + P],
                rhs=wq[:, WCOL * gx + c0: WCOL * gx + c0 + n].bitcast(FP8X4),
                rhs_scale=ws[:, WCOL * gx + c0: WCOL * gx + c0 + n],
                start=start,
                stop=stop,
            )

        accs = {}

        def mm(m, g):
            acc = ps.tile([P, 512], F32, name=M_RING[(N_G * m + g) % len(M_RING)])
            mx(m, acc[:], g, 0, 512, True, False)
            mx(m, acc[:, 0:P], (g - 1) % N_G, 512, P, False, True)
            accs[(m, g)] = acc

        outs = {}

        def ev(m, g):
            if m not in outs:
                outs[m] = op.tile([P, OUT_F], F32, name="ot")
            ot = outs[m]
            acc = accs[(m, g)]
            n = GP_COLS.get((m, g), 0)

            def add_bias(add, src, lo, hi):
                for a, z, c in ((0, SHIFT, OUT_F - SHIFT), (SHIFT, 512, 0)) if g == 0 else ((0, 512, 512 * g - SHIFT),):
                    a = max(a, lo)
                    z = min(z, hi)
                    if a < z:
                        d = c + a - (SHIFT if g == 0 and a >= SHIFT else 0)
                        add(out=ot[:, d: d + z - a], in0=src[:, a:z], in1=bias[:, d: d + z - a], op=ADD)

            if n > 0:
                st = stp.tile([P, n], F32, name="st%d" % n)
                nc.scalar.copy(out=st[:], in_=acc[:, 0:n])
                add_bias(nc.gpsimd.tensor_tensor, st, 0, n)
            if n < 512:
                add_bias(nc.vector.tensor_tensor, acc, n, 512)

        def store(m, c0, c1):
            nc.sync.dma_start(out=out[P * m: P * m + P, c0:c1], in_=outs[m][:, c0:c1])

        xt(0)
        xc(0)
        w_t(0)
        w_h(3)
        w_h(0)
        w_t(1)
        w_h(1)
        bias_mm(0)
        bias_mm(1)
        wa(0, nc.scalar.copy)
        wb(0, nc.scalar.copy)
        xquant(0)
        wc(3, nc.vector.tensor_copy)
        wc(0, nc.vector.tensor_copy)
        qa(0)
        qc(3)
        wa(1, nc.vector.tensor_copy)
        qb(0)
        wb(1, nc.scalar.copy)
        w_t(2)
        w_h(2)
        bias_copy(0, nc.scalar.copy)
        bias_copy(1, nc.scalar.copy)
        wa(2, nc.scalar.copy)
        mm(0, 0)
        w_t(3)
        qc(0)
        wc(1, nc.vector.tensor_copy)
        qab(1)
        mm(0, 1)
        wb(2, nc.scalar.copy)
        wa(3, nc.scalar.copy)
        wc(2, nc.vector.tensor_copy)
        qc(1)
        xt(1)
        ev(0, 0)
        qab(2)
        qc(2)
        mm(0, 2)
        wb(3, nc.scalar.copy)
        xt(2)
        xc(1)
        ev(0, 1)
        qab(3)
        mm(0, 3)
        store(0, 0, 960)
        xquant(1)
        xc(2)
        ev(0, 2)
        ev(0, 3)
        store(0, 960, 2048)

        for m in range(1, N_M):
            if m + 1 < N_M:
                xquant(m + 1)
            for g in range(N_G):
                mm(m, g)
            ev(m, 0)
            ev(m, 1)
            if m + 2 < N_M:
                xt(m + 2)
            if m + 2 < N_M:
                xc(m + 2)
            store(m, 0, 960)
            ev(m, 2)
            ev(m, 3)
            store(m, 960, 2048)
